import numpy as np
import ml_dtypes

BF16 = ml_dtypes.bfloat16


def bf(x):
    return np.asarray(x, np.float32).astype(BF16)


def f32(x):
    return np.asarray(x, np.float32)


def f64(x):
    return np.asarray(x).astype(np.float64)


def striped(idx):
    return np.tile(idx.reshape(-1, 16).T, (8, 1))


C, S, N, R, E = 128, 512, 128, 512, 512


def setup_inputs():
    return {"x": f32(np.random.standard_normal((C, S))), "sel": f32(np.random.uniform(0.0, 1.0, (C, N))), "mk": bf(np.random.standard_normal((C, R))), "shrink": f32(0.9 + 0.2 * np.random.uniform(0.0, 1.0, (R, 1))), "mv": bf(np.random.standard_normal((R, E))), "offs": striped(np.random.permutation(S)[:N])}


def reference(x, sel, mk, shrink, mv, offs):
    idx = offs[:16].T.reshape(-1)
    q = f64(x)[:, idx]
    u = q * f64(sel)
    bsq = np.sum(q * u, axis=0, keepdims=True)
    keys = np.concatenate([f64(mk) * f64(mk), f64(mk)], axis=0)
    qs = np.concatenate([-f64(sel), 2.0 * u], axis=0)
    sim = (keys.T @ qs - bsq) * f64(shrink) / np.sqrt(C)
    ex = np.exp(sim - sim.max(axis=0, keepdims=True))
    aff = ex / ex.sum(axis=0, keepdims=True)
    return f64(mv).T @ aff

@@ -1,0 +1,106 @@
+import math
+
+import concourse.mybir as mybir
+from concourse.masks import make_identity
+
+FP32 = mybir.dt.float32
+BF16 = mybir.dt.bfloat16
+U16 = mybir.dt.uint16
+ALU = mybir.AluOpType
+FUNC = mybir.ActivationFunctionType
+AXIS = mybir.AxisListType
+
+P = 128
+C, S, N, R, E = 128, 512, 128, 512, 512
+R_BLOCKS = R // P
+E_BLOCKS = E // P
+
+FLOPS = 2 * (2 * C + C) * R * N + 2 * R * E * N
+
+
+def tile_vidsam_kernel(tc, x, sel, mk, shrink, mv, offs, out):
+    nc = tc.nc
+    with (
+        tc.tile_pool(name="held", bufs=1) as held,
+        tc.tile_pool(name="work", bufs=1) as work,
+        tc.tile_pool(name="staged", bufs=E_BLOCKS) as staged,
+        tc.psum_pool(name="psum", bufs=1) as psum,
+        tc.psum_pool(name="psum_out", bufs=E_BLOCKS) as psum_out,
+    ):
+        offsets = held.tile([P, N // 16], U16, name="offsets")
+        nc.sync.dma_start(offsets[:], offs)
+        x_sb = held.tile([C, S], FP32, name="x_sb")
+        nc.sync.dma_start(x_sb[:], x)
+        mk_sb = held.tile([C, R], BF16, name="mk_sb")
+        nc.scalar.dma_start(mk_sb[:], mk)
+        sel_sb = held.tile([C, N], FP32, name="sel_sb")
+        nc.scalar.dma_start(sel_sb[:], sel)
+        shrink_rows = held.tile([P, R], FP32, name="shrink_rows")
+        nc.scalar.dma_start(shrink_rows[:], shrink.rearrange("r one -> (r one)").partition_broadcast(P))
+        mv_sb = held.tile([P, R_BLOCKS, E], BF16, name="mv_sb")
+        nc.sync.dma_start(mv_sb[:], mv.rearrange("(b p) e -> p b e", p=P))
+
+        identity = held.tile([P, P], BF16, name="identity")
+        make_identity(nc, identity[:])
+        ones = held.tile([C, R], BF16, name="ones")
+        nc.gpsimd.memset(ones[:], 1.0)
+        warm = held.tile([P, 1], FP32, name="warm")
+        nc.vector.memset(warm[:], 0.0)
+        nc.scalar.activation(warm[:], warm[:], FUNC.Exp)
+
+        mk_sq = work.tile([C, R], BF16, name="mk_sq")
+        nc.vector.tensor_tensor(mk_sq[:], mk_sb[:], mk_sb[:], ALU.mult)
+        sel_bf = work.tile([C, N], BF16, name="sel_bf")
+        nc.scalar.copy(sel_bf[:], sel_sb[:])
+        scale_rows = work.tile([P, R], FP32, name="scale_rows")
+        nc.gpsimd.tensor_scalar_mul(scale_rows[:], shrink_rows[:], 1.0 / math.sqrt(C))
+
+        u = work.tile([C, N], FP32, name="u")
+        nc.vector.tensor_tensor(u[:], x_sb[:].indirect(offsets[:]), sel_sb[:], ALU.mult)
+        u_minus2 = work.tile([C, N], BF16, name="u_minus2")
+        nc.vector.tensor_scalar_mul(u_minus2[:], u[:], -2.0)
+        xu = work.tile([C, N], FP32, name="xu")
+        nc.vector.tensor_tensor(xu[:], x_sb[:].indirect(offsets[:]), u[:], ALU.mult)
+        xu_bf = work.tile([C, N], BF16, name="xu_bf")
+        nc.vector.tensor_copy(xu_bf[:], xu[:])
+
+        dist = psum.tile([N, R], FP32, name="dist")
+        nc.tensor.matmul(dist[:], sel_bf[:], mk_sq[:], start=True, stop=False)
+        nc.tensor.matmul(dist[:], u_minus2[:], mk_sb[:], start=False, stop=False)
+        nc.tensor.matmul(dist[:], xu_bf[:], ones[:], start=False, stop=True)
+
+        neg_sim = work.tile([N, R], FP32, name="neg_sim")
+        nc.vector.tensor_tensor(neg_sim[:], dist[:], scale_rows[:], ALU.mult)
+        smallest = work.tile([N, 1], FP32, name="smallest")
+        nc.vector.tensor_reduce(smallest[:], neg_sim[:], AXIS.X, ALU.min)
+        expo = work.tile([N, R], FP32, name="expo")
+        total = work.tile([N, 1], FP32, name="total")
+        nc.scalar.activation(expo[:], neg_sim[:], FUNC.Exp, bias=smallest[:], scale=-1.0, accum_out=total[:])
+        inv_total = work.tile([N, 1], FP32, name="inv_total")
+        nc.vector.reciprocal(inv_total[:], total[:])
+        aff = work.tile([N, R], BF16, name="aff")
+        nc.vector.tensor_scalar_mul(aff[:], expo[:], inv_total[:])
+
+        aff_t_ps = psum.tile([P, R_BLOCKS, N], BF16, name="aff_t_ps")
+        for b in range(R_BLOCKS):
+            nc.tensor.transpose(aff_t_ps[:, b, :], aff[:, b * P : (b + 1) * P], identity[:])
+        aff_t = work.tile([P, R_BLOCKS, N], BF16, name="aff_t")
+        nc.vector.tensor_copy(aff_t[:], aff_t_ps[:])
+
+        for e in range(E_BLOCKS):
+            acc = psum_out.tile([P, N], FP32, name="acc")
+            for b in range(R_BLOCKS):
+                nc.tensor.matmul(
+                    acc[:],
+                    mv_sb[:, b, e * P : (e + 1) * P],
+                    aff_t[:, b, :],
+                    start=(b == 0),
+                    stop=(b == R_BLOCKS - 1),
+                )
+            block = staged.tile([P, N], FP32, name="block")
+            if e % 2 == 0:
+                nc.vector.tensor_copy(block[:], acc[:])
+                nc.sync.dma_start(out[e * P : (e + 1) * P, :], block[:])
+            else:
+                nc.scalar.copy(block[:], acc[:])
+                nc.scalar.dma_start(out[e * P : (e + 1) * P, :], block[:])

@@ -15,7 +15,7 @@ C, S, N, R, E = 128, 512, 128, 512, 512
 R_BLOCKS = R // P
 E_BLOCKS = E // P
 
-FLOPS = 2 * (2 * C + C) * R * N + 2 * R * E * N
+FLOPS = 2 * (2 * C) * R * N + 2 * C * N + 2 * R * E * N
 
 
 def tile_vidsam_kernel(tc, x, sel, mk, shrink, mv, offs, out):
@@ -36,13 +36,13 @@ def tile_vidsam_kernel(tc, x, sel, mk, shrink, mv, offs, out):
         sel_sb = held.tile([C, N], FP32, name="sel_sb")
         nc.scalar.dma_start(sel_sb[:], sel)
         shrink_rows = held.tile([P, R], FP32, name="shrink_rows")
-        nc.scalar.dma_start(shrink_rows[:], shrink.rearrange("r one -> (r one)").partition_broadcast(P))
+        nc.gpsimd.dma_start(shrink_rows[:], shrink.rearrange("r one -> (r one)").partition_broadcast(P))
         mv_sb = held.tile([P, R_BLOCKS, E], BF16, name="mv_sb")
         nc.sync.dma_start(mv_sb[:], mv.rearrange("(b p) e -> p b e", p=P))
 
         identity = held.tile([P, P], BF16, name="identity")
         make_identity(nc, identity[:])
-        ones = held.tile([C, R], BF16, name="ones")
+        ones = held.tile([C, 1], BF16, name="ones")
         nc.gpsimd.memset(ones[:], 1.0)
         warm = held.tile([P, 1], FP32, name="warm")
         nc.vector.memset(warm[:], 0.0)
@@ -53,7 +53,7 @@ def tile_vidsam_kernel(tc, x, sel, mk, shrink, mv, offs, out):
         sel_bf = work.tile([C, N], BF16, name="sel_bf")
         nc.scalar.copy(sel_bf[:], sel_sb[:])
         scale_rows = work.tile([P, R], FP32, name="scale_rows")
-        nc.gpsimd.tensor_scalar_mul(scale_rows[:], shrink_rows[:], 1.0 / math.sqrt(C))
+        nc.scalar.mul(scale_rows[:], shrink_rows[:], 1.0 / math.sqrt(C))
 
         u = work.tile([C, N], FP32, name="u")
         nc.vector.tensor_tensor(u[:], x_sb[:].indirect(offsets[:]), sel_sb[:], ALU.mult)
@@ -64,13 +64,14 @@ def tile_vidsam_kernel(tc, x, sel, mk, shrink, mv, offs, out):
         xu_bf = work.tile([C, N], BF16, name="xu_bf")
         nc.vector.tensor_copy(xu_bf[:], xu[:])
 
-        dist = psum.tile([N, R], FP32, name="dist")
-        nc.tensor.matmul(dist[:], sel_bf[:], mk_sq[:], start=True, stop=False)
-        nc.tensor.matmul(dist[:], u_minus2[:], mk_sb[:], start=False, stop=False)
-        nc.tensor.matmul(dist[:], xu_bf[:], ones[:], start=False, stop=True)
+        cross = psum.tile([N, R], FP32, name="cross")
+        nc.tensor.matmul(cross[:], sel_bf[:], mk_sq[:], start=True, stop=False)
+        nc.tensor.matmul(cross[:], u_minus2[:], mk_sb[:], start=False, stop=True)
+        bsq = psum.tile([N, 1], FP32, name="bsq")
+        nc.tensor.matmul(bsq[:], xu_bf[:], ones[:], start=True, stop=True)
 
         neg_sim = work.tile([N, R], FP32, name="neg_sim")
-        nc.vector.tensor_tensor(neg_sim[:], dist[:], scale_rows[:], ALU.mult)
+        nc.vector.scalar_tensor_tensor(neg_sim[:], cross[:], bsq[:], scale_rows[:], ALU.add, ALU.mult)
         smallest = work.tile([N, 1], FP32, name="smallest")
         nc.vector.tensor_reduce(smallest[:], neg_sim[:], AXIS.X, ALU.min)
         expo = work.tile([N, R], FP32, name="expo")

@@ -36,7 +36,7 @@ def tile_vidsam_kernel(tc, x, sel, mk, shrink, mv, offs, out):
         sel_sb = held.tile([C, N], FP32, name="sel_sb")
         nc.scalar.dma_start(sel_sb[:], sel)
         shrink_rows = held.tile([P, R], FP32, name="shrink_rows")
-        nc.gpsimd.dma_start(shrink_rows[:], shrink.rearrange("r one -> (r one)").partition_broadcast(P))
+        nc.sync.dma_start(shrink_rows[:], shrink.rearrange("r one -> (r one)").partition_broadcast(P))
         mv_sb = held.tile([P, R_BLOCKS, E], BF16, name="mv_sb")
         nc.sync.dma_start(mv_sb[:], mv.rearrange("(b p) e -> p b e", p=P))
 
@@ -51,7 +51,7 @@ def tile_vidsam_kernel(tc, x, sel, mk, shrink, mv, offs, out):
         mk_sq = work.tile([C, R], BF16, name="mk_sq")
         nc.vector.tensor_tensor(mk_sq[:], mk_sb[:], mk_sb[:], ALU.mult)
         sel_bf = work.tile([C, N], BF16, name="sel_bf")
-        nc.scalar.copy(sel_bf[:], sel_sb[:])
+        nc.vector.tensor_copy(sel_bf[:], sel_sb[:])
         scale_rows = work.tile([P, R], FP32, name="scale_rows")
         nc.scalar.mul(scale_rows[:], shrink_rows[:], 1.0 / math.sqrt(C))
 

@@ -14,6 +14,9 @@ P = 128
 C, S, N, R, E = 128, 512, 128, 512, 512
 R_BLOCKS = R // P
 E_BLOCKS = E // P
+HALVES = 2
+HALF_BLOCKS = R_BLOCKS // HALVES
+PSUM_BANKS = 8
 
 FLOPS = 2 * (2 * C) * R * N + 2 * C * N + 2 * R * E * N
 
@@ -24,8 +27,7 @@ def tile_vidsam_kernel(tc, x, sel, mk, shrink, mv, offs, out):
         tc.tile_pool(name="held", bufs=1) as held,
         tc.tile_pool(name="work", bufs=1) as work,
         tc.tile_pool(name="staged", bufs=E_BLOCKS) as staged,
-        tc.psum_pool(name="psum", bufs=1) as psum,
-        tc.psum_pool(name="psum_out", bufs=E_BLOCKS) as psum_out,
+        tc.psum_pool(name="banks", bufs=PSUM_BANKS) as banks,
     ):
         offsets = held.tile([P, N // 16], U16, name="offsets")
         nc.sync.dma_start(offsets[:], offs)
@@ -42,6 +44,8 @@ def tile_vidsam_kernel(tc, x, sel, mk, shrink, mv, offs, out):
 
         identity = held.tile([P, P], BF16, name="identity")
         make_identity(nc, identity[:])
+        identity_f32 = held.tile([P, P], FP32, name="identity_f32")
+        make_identity(nc, identity_f32[:])
         ones = held.tile([C, 1], BF16, name="ones")
         nc.gpsimd.memset(ones[:], 1.0)
         warm = held.tile([P, 1], FP32, name="warm")
@@ -64,44 +68,59 @@ def tile_vidsam_kernel(tc, x, sel, mk, shrink, mv, offs, out):
         xu_bf = work.tile([C, N], BF16, name="xu_bf")
         nc.vector.tensor_copy(xu_bf[:], xu[:])
 
-        cross = psum.tile([N, R], FP32, name="cross")
+        cross = banks.tile([N, R], FP32, name="cross", tag="bank")
         nc.tensor.matmul(cross[:], sel_bf[:], mk_sq[:], start=True, stop=False)
         nc.tensor.matmul(cross[:], u_minus2[:], mk_sb[:], start=False, stop=True)
-        bsq = psum.tile([N, 1], FP32, name="bsq")
+        bsq = banks.tile([N, 1], FP32, name="bsq", tag="bank")
         nc.tensor.matmul(bsq[:], xu_bf[:], ones[:], start=True, stop=True)
 
         neg_sim = work.tile([N, R], FP32, name="neg_sim")
         nc.vector.scalar_tensor_tensor(neg_sim[:], cross[:], bsq[:], scale_rows[:], ALU.add, ALU.mult)
         smallest = work.tile([N, 1], FP32, name="smallest")
         nc.vector.tensor_reduce(smallest[:], neg_sim[:], AXIS.X, ALU.min)
-        expo = work.tile([N, R], FP32, name="expo")
+
+        expo = work.tile([N, R], BF16, name="expo")
+        half_totals = work.tile([N, HALVES], FP32, name="half_totals")
+        expo_t = work.tile([P, R_BLOCKS, N], BF16, name="expo_t")
+        expo_t_ps = [banks.tile([P, HALF_BLOCKS, N], BF16, name=f"expo_t_ps{h}", tag="bank") for h in range(HALVES)]
+        for h in range(HALVES):
+            slots = slice(h * R // HALVES, (h + 1) * R // HALVES)
+            nc.scalar.activation(
+                expo[:, slots],
+                neg_sim[:, slots],
+                FUNC.Exp,
+                bias=smallest[:],
+                scale=-1.0,
+                accum_out=half_totals[:, h : h + 1],
+            )
+        for h in range(HALVES):
+            for k in range(HALF_BLOCKS):
+                b = h * HALF_BLOCKS + k
+                nc.tensor.transpose(expo_t_ps[h][:, k, :], expo[:, b * P : (b + 1) * P], identity[:])
+            nc.scalar.copy(expo_t[:, h * HALF_BLOCKS : (h + 1) * HALF_BLOCKS, :], expo_t_ps[h][:])
+
         total = work.tile([N, 1], FP32, name="total")
-        nc.scalar.activation(expo[:], neg_sim[:], FUNC.Exp, bias=smallest[:], scale=-1.0, accum_out=total[:])
+        nc.vector.tensor_reduce(total[:], half_totals[:], AXIS.X, ALU.add)
         inv_total = work.tile([N, 1], FP32, name="inv_total")
         nc.vector.reciprocal(inv_total[:], total[:])
-        aff = work.tile([N, R], BF16, name="aff")
-        nc.vector.tensor_scalar_mul(aff[:], expo[:], inv_total[:])
-
-        aff_t_ps = psum.tile([P, R_BLOCKS, N], BF16, name="aff_t_ps")
-        for b in range(R_BLOCKS):
-            nc.tensor.transpose(aff_t_ps[:, b, :], aff[:, b * P : (b + 1) * P], identity[:])
-        aff_t = work.tile([P, R_BLOCKS, N], BF16, name="aff_t")
-        nc.vector.tensor_copy(aff_t[:], aff_t_ps[:])
+        inv_cols = work.tile([N, P], FP32, name="inv_cols")
+        nc.vector.tensor_copy(inv_cols[:], inv_total[:].to_broadcast([N, P]))
+        inv_rows_ps = banks.tile([P, N], FP32, name="inv_rows_ps", tag="bank")
+        nc.tensor.transpose(inv_rows_ps[:], inv_cols[:], identity_f32[:])
+        inv_rows = work.tile([P, N], FP32, name="inv_rows")
+        nc.scalar.copy(inv_rows[:], inv_rows_ps[:])
 
         for e in range(E_BLOCKS):
-            acc = psum_out.tile([P, N], FP32, name="acc")
+            acc = banks.tile([P, N], FP32, name="acc", tag="bank")
             for b in range(R_BLOCKS):
                 nc.tensor.matmul(
                     acc[:],
                     mv_sb[:, b, e * P : (e + 1) * P],
-                    aff_t[:, b, :],
+                    expo_t[:, b, :],
                     start=(b == 0),
                     stop=(b == R_BLOCKS - 1),
                 )
             block = staged.tile([P, N], FP32, name="block")
-            if e % 2 == 0:
-                nc.vector.tensor_copy(block[:], acc[:])
-                nc.sync.dma_start(out[e * P : (e + 1) * P, :], block[:])
-            else:
-                nc.scalar.copy(block[:], acc[:])
-                nc.scalar.dma_start(out[e * P : (e + 1) * P, :], block[:])
+            nc.vector.tensor_tensor(block[:], acc[:], inv_rows[:], ALU.mult)
+            queue = nc.sync if e % 2 == 0 else nc.scalar
+            queue.dma_start(out[e * P : (e + 1) * P, :], block[:])

@@ -80,27 +80,17 @@ def tile_vidsam_kernel(tc, x, sel, mk, shrink, mv, offs, out):
         nc.vector.tensor_reduce(smallest[:], neg_sim[:], AXIS.X, ALU.min)
 
         expo = work.tile([N, R], BF16, name="expo")
-        half_totals = work.tile([N, HALVES], FP32, name="half_totals")
+        total = work.tile([N, 1], FP32, name="total")
+        nc.scalar.activation(expo[:], neg_sim[:], FUNC.Exp, bias=smallest[:], scale=-1.0, accum_out=total[:])
+
         expo_t = work.tile([P, R_BLOCKS, N], BF16, name="expo_t")
-        expo_t_ps = [banks.tile([P, HALF_BLOCKS, N], BF16, name=f"expo_t_ps{h}", tag="bank") for h in range(HALVES)]
         for h in range(HALVES):
-            slots = slice(h * R // HALVES, (h + 1) * R // HALVES)
-            nc.scalar.activation(
-                expo[:, slots],
-                neg_sim[:, slots],
-                FUNC.Exp,
-                bias=smallest[:],
-                scale=-1.0,
-                accum_out=half_totals[:, h : h + 1],
-            )
-        for h in range(HALVES):
+            expo_t_ps = banks.tile([P, HALF_BLOCKS, N], BF16, name="expo_t_ps", tag="bank")
             for k in range(HALF_BLOCKS):
                 b = h * HALF_BLOCKS + k
-                nc.tensor.transpose(expo_t_ps[h][:, k, :], expo[:, b * P : (b + 1) * P], identity[:])
-            nc.scalar.copy(expo_t[:, h * HALF_BLOCKS : (h + 1) * HALF_BLOCKS, :], expo_t_ps[h][:])
+                nc.tensor.transpose(expo_t_ps[:, k, :], expo[:, b * P : (b + 1) * P], identity[:])
+            nc.scalar.copy(expo_t[:, h * HALF_BLOCKS : (h + 1) * HALF_BLOCKS, :], expo_t_ps[:])
 
-        total = work.tile([N, 1], FP32, name="total")
-        nc.vector.tensor_reduce(total[:], half_totals[:], AXIS.X, ALU.add)
         inv_total = work.tile([N, 1], FP32, name="inv_total")
         nc.vector.reciprocal(inv_total[:], total[:])
         inv_cols = work.tile([N, P], FP32, name="inv_cols")

@@ -17,6 +17,7 @@ E_BLOCKS = E // P
 HALVES = 2
 HALF_BLOCKS = R_BLOCKS // HALVES
 PSUM_BANKS = 8
+INV_SQRT_C = 1.0 / math.sqrt(C)
 
 FLOPS = 2 * (2 * C) * R * N + 2 * C * N + 2 * R * E * N
 
@@ -56,8 +57,6 @@ def tile_vidsam_kernel(tc, x, sel, mk, shrink, mv, offs, out):
         nc.vector.tensor_tensor(mk_sq[:], mk_sb[:], mk_sb[:], ALU.mult)
         sel_bf = work.tile([C, N], BF16, name="sel_bf")
         nc.vector.tensor_copy(sel_bf[:], sel_sb[:])
-        scale_rows = work.tile([P, R], FP32, name="scale_rows")
-        nc.scalar.mul(scale_rows[:], shrink_rows[:], 1.0 / math.sqrt(C))
 
         u = work.tile([C, N], FP32, name="u")
         nc.vector.tensor_tensor(u[:], x_sb[:].indirect(offsets[:]), sel_sb[:], ALU.mult)
@@ -74,14 +73,16 @@ def tile_vidsam_kernel(tc, x, sel, mk, shrink, mv, offs, out):
         bsq = banks.tile([N, 1], FP32, name="bsq", tag="bank")
         nc.tensor.matmul(bsq[:], xu_bf[:], ones[:], start=True, stop=True)
 
-        neg_sim = work.tile([N, R], FP32, name="neg_sim")
-        nc.vector.scalar_tensor_tensor(neg_sim[:], cross[:], bsq[:], scale_rows[:], ALU.add, ALU.mult)
+        dist = work.tile([N, R], FP32, name="dist")
+        nc.vector.scalar_tensor_tensor(dist[:], cross[:], bsq[:], shrink_rows[:], ALU.add, ALU.mult)
         smallest = work.tile([N, 1], FP32, name="smallest")
-        nc.vector.tensor_reduce(smallest[:], neg_sim[:], AXIS.X, ALU.min)
+        nc.vector.tensor_reduce(smallest[:], dist[:], AXIS.X, ALU.min)
+        shift = work.tile([N, 1], FP32, name="shift")
+        nc.scalar.mul(shift[:], smallest[:], INV_SQRT_C)
 
         expo = work.tile([N, R], BF16, name="expo")
         total = work.tile([N, 1], FP32, name="total")
-        nc.scalar.activation(expo[:], neg_sim[:], FUNC.Exp, bias=smallest[:], scale=-1.0, accum_out=total[:])
+        nc.scalar.activation(expo[:], dist[:], FUNC.Exp, bias=shift[:], scale=-INV_SQRT_C, accum_out=total[:])
 
         expo_t = work.tile([P, R_BLOCKS, N], BF16, name="expo_t")
         for h in range(HALVES):

@@ -56,12 +56,14 @@ def tile_vidsam_kernel(tc, x, sel, mk, shrink, mv, offs, out):
         mk_sq = work.tile([C, R], BF16, name="mk_sq")
         nc.vector.tensor_tensor(mk_sq[:], mk_sb[:], mk_sb[:], ALU.mult)
         sel_bf = work.tile([C, N], BF16, name="sel_bf")
-        nc.vector.tensor_copy(sel_bf[:], sel_sb[:])
+        nc.scalar.copy(sel_bf[:], sel_sb[:])
 
         u = work.tile([C, N], FP32, name="u")
         nc.vector.tensor_tensor(u[:], x_sb[:].indirect(offsets[:]), sel_sb[:], ALU.mult)
         u_minus2 = work.tile([C, N], BF16, name="u_minus2")
-        nc.vector.tensor_scalar_mul(u_minus2[:], u[:], -2.0)
+        nc.scalar.mul(u_minus2[:], u[:], -2.0)
+        shrink_scaled = held.tile([P, R], FP32, name="shrink_scaled")
+        nc.scalar.mul(shrink_scaled[:], shrink_rows[:], INV_SQRT_C)
         xu = work.tile([C, N], FP32, name="xu")
         nc.vector.tensor_tensor(xu[:], x_sb[:].indirect(offsets[:]), u[:], ALU.mult)
         xu_bf = work.tile([C, N], BF16, name="xu_bf")
@@ -74,15 +76,13 @@ def tile_vidsam_kernel(tc, x, sel, mk, shrink, mv, offs, out):
         nc.tensor.matmul(bsq[:], xu_bf[:], ones[:], start=True, stop=True)
 
         dist = work.tile([N, R], FP32, name="dist")
-        nc.vector.scalar_tensor_tensor(dist[:], cross[:], bsq[:], shrink_rows[:], ALU.add, ALU.mult)
+        nc.vector.scalar_tensor_tensor(dist[:], cross[:], bsq[:], shrink_scaled[:], ALU.add, ALU.mult)
         smallest = work.tile([N, 1], FP32, name="smallest")
         nc.vector.tensor_reduce(smallest[:], dist[:], AXIS.X, ALU.min)
-        shift = work.tile([N, 1], FP32, name="shift")
-        nc.scalar.mul(shift[:], smallest[:], INV_SQRT_C)
 
         expo = work.tile([N, R], BF16, name="expo")
         total = work.tile([N, 1], FP32, name="total")
-        nc.scalar.activation(expo[:], dist[:], FUNC.Exp, bias=shift[:], scale=-INV_SQRT_C, accum_out=total[:])
+        nc.scalar.activation(expo[:], dist[:], FUNC.Exp, bias=smallest[:], scale=-1.0, accum_out=total[:])
 
         expo_t = work.tile([P, R_BLOCKS, N], BF16, name="expo_t")
         for h in range(HALVES):

@@ -81,17 +81,30 @@ def tile_vidsam_kernel(tc, x, sel, mk, shrink, mv, offs, out):
         nc.vector.tensor_reduce(smallest[:], dist[:], AXIS.X, ALU.min)
 
         expo = work.tile([N, R], BF16, name="expo")
-        total = work.tile([N, 1], FP32, name="total")
-        nc.scalar.activation(expo[:], dist[:], FUNC.Exp, bias=smallest[:], scale=-1.0, accum_out=total[:])
+        block_totals = work.tile([N, R_BLOCKS], FP32, name="block_totals")
+        for b in range(R_BLOCKS):
+            nc.scalar.activation(
+                expo[:, b * P : (b + 1) * P],
+                dist[:, b * P : (b + 1) * P],
+                FUNC.Exp,
+                bias=smallest[:],
+                scale=-1.0,
+                accum_out=block_totals[:, b : b + 1],
+            )
 
         expo_t = work.tile([P, R_BLOCKS, N], BF16, name="expo_t")
-        for h in range(HALVES):
-            expo_t_ps = banks.tile([P, HALF_BLOCKS, N], BF16, name="expo_t_ps", tag="bank")
-            for k in range(HALF_BLOCKS):
-                b = h * HALF_BLOCKS + k
-                nc.tensor.transpose(expo_t_ps[:, k, :], expo[:, b * P : (b + 1) * P], identity[:])
-            nc.scalar.copy(expo_t[:, h * HALF_BLOCKS : (h + 1) * HALF_BLOCKS, :], expo_t_ps[:])
+        for b in range(R_BLOCKS):
+            expo_t_ps = banks.tile([P, N], BF16, name="expo_t_ps", tag="bank")
+            nc.tensor.transpose(expo_t_ps[:], expo[:, b * P : (b + 1) * P], identity[:])
+            nc.vector.tensor_copy(expo_t[:, b, :], expo_t_ps[:])
 
+        acc = [banks.tile([P, N], FP32, name="acc%d" % e, tag="bank") for e in range(E_BLOCKS)]
+        for b in range(HALF_BLOCKS):
+            for e in range(E_BLOCKS):
+                nc.tensor.matmul(acc[e][:], mv_sb[:, b, e * P : (e + 1) * P], expo_t[:, b, :], start=(b == 0), stop=False)
+
+        total = work.tile([N, 1], FP32, name="total")
+        nc.vector.tensor_reduce(total[:], block_totals[:], AXIS.X, ALU.add)
         inv_total = work.tile([N, 1], FP32, name="inv_total")
         nc.vector.reciprocal(inv_total[:], total[:])
         inv_cols = work.tile([N, P], FP32, name="inv_cols")
@@ -102,16 +115,11 @@ def tile_vidsam_kernel(tc, x, sel, mk, shrink, mv, offs, out):
         nc.scalar.copy(inv_rows[:], inv_rows_ps[:])
 
         for e in range(E_BLOCKS):
-            acc = banks.tile([P, N], FP32, name="acc", tag="bank")
-            for b in range(R_BLOCKS):
+            for b in range(HALF_BLOCKS, R_BLOCKS):
                 nc.tensor.matmul(
-                    acc[:],
-                    mv_sb[:, b, e * P : (e + 1) * P],
-                    expo_t[:, b, :],
-                    start=(b == 0),
-                    stop=(b == R_BLOCKS - 1),
+                    acc[e][:], mv_sb[:, b, e * P : (e + 1) * P], expo_t[:, b, :], start=False, stop=(b == R_BLOCKS - 1)
                 )
             block = staged.tile([P, N], FP32, name="block")
-            nc.vector.tensor_tensor(block[:], acc[:], inv_rows[:], ALU.mult)
+            nc.vector.tensor_tensor(block[:], acc[e][:], inv_rows[:], ALU.mult)
             queue = nc.sync if e % 2 == 0 else nc.scalar
             queue.dma_start(out[e * P : (e + 1) * P, :], block[:])

@@ -56,14 +56,12 @@ def tile_vidsam_kernel(tc, x, sel, mk, shrink, mv, offs, out):
         mk_sq = work.tile([C, R], BF16, name="mk_sq")
         nc.vector.tensor_tensor(mk_sq[:], mk_sb[:], mk_sb[:], ALU.mult)
         sel_bf = work.tile([C, N], BF16, name="sel_bf")
-        nc.scalar.copy(sel_bf[:], sel_sb[:])
+        nc.vector.tensor_copy(sel_bf[:], sel_sb[:])
 
         u = work.tile([C, N], FP32, name="u")
         nc.vector.tensor_tensor(u[:], x_sb[:].indirect(offsets[:]), sel_sb[:], ALU.mult)
         u_minus2 = work.tile([C, N], BF16, name="u_minus2")
-        nc.scalar.mul(u_minus2[:], u[:], -2.0)
-        shrink_scaled = held.tile([P, R], FP32, name="shrink_scaled")
-        nc.scalar.mul(shrink_scaled[:], shrink_rows[:], INV_SQRT_C)
+        nc.vector.tensor_scalar_mul(u_minus2[:], u[:], -2.0)
         xu = work.tile([C, N], FP32, name="xu")
         nc.vector.tensor_tensor(xu[:], x_sb[:].indirect(offsets[:]), u[:], ALU.mult)
         xu_bf = work.tile([C, N], BF16, name="xu_bf")
@@ -76,9 +74,11 @@ def tile_vidsam_kernel(tc, x, sel, mk, shrink, mv, offs, out):
         nc.tensor.matmul(bsq[:], xu_bf[:], ones[:], start=True, stop=True)
 
         dist = work.tile([N, R], FP32, name="dist")
-        nc.vector.scalar_tensor_tensor(dist[:], cross[:], bsq[:], shrink_scaled[:], ALU.add, ALU.mult)
+        nc.vector.scalar_tensor_tensor(dist[:], cross[:], bsq[:], shrink_rows[:], ALU.add, ALU.mult)
         smallest = work.tile([N, 1], FP32, name="smallest")
         nc.vector.tensor_reduce(smallest[:], dist[:], AXIS.X, ALU.min)
+        shift = work.tile([N, 1], FP32, name="shift")
+        nc.scalar.mul(shift[:], smallest[:], INV_SQRT_C)
 
         expo = work.tile([N, R], BF16, name="expo")
         block_totals = work.tile([N, R_BLOCKS], FP32, name="block_totals")
@@ -87,8 +87,8 @@ def tile_vidsam_kernel(tc, x, sel, mk, shrink, mv, offs, out):
                 expo[:, b * P : (b + 1) * P],
                 dist[:, b * P : (b + 1) * P],
                 FUNC.Exp,
-                bias=smallest[:],
-                scale=-1.0,
+                bias=shift[:],
+                scale=-INV_SQRT_C,
                 accum_out=block_totals[:, b : b + 1],
             )
 

@@ -14,8 +14,6 @@ P = 128
 C, S, N, R, E = 128, 512, 128, 512, 512
 R_BLOCKS = R // P
 E_BLOCKS = E // P
-HALVES = 2
-HALF_BLOCKS = R_BLOCKS // HALVES
 PSUM_BANKS = 8
 INV_SQRT_C = 1.0 / math.sqrt(C)
 
@@ -49,6 +47,8 @@ def tile_vidsam_kernel(tc, x, sel, mk, shrink, mv, offs, out):
         make_identity(nc, identity_f32[:])
         ones = held.tile([C, 1], BF16, name="ones")
         nc.gpsimd.memset(ones[:], 1.0)
+        minus_ones = held.tile([N, P], BF16, name="minus_ones")
+        nc.gpsimd.memset(minus_ones[:], -1.0)
         warm = held.tile([P, 1], FP32, name="warm")
         nc.vector.memset(warm[:], 0.0)
         nc.scalar.activation(warm[:], warm[:], FUNC.Exp)
@@ -75,50 +75,47 @@ def tile_vidsam_kernel(tc, x, sel, mk, shrink, mv, offs, out):
 
         dist = work.tile([N, R], FP32, name="dist")
         nc.vector.scalar_tensor_tensor(dist[:], cross[:], bsq[:], shrink_rows[:], ALU.add, ALU.mult)
-        smallest = work.tile([N, 1], FP32, name="smallest")
-        nc.vector.tensor_reduce(smallest[:], dist[:], AXIS.X, ALU.min)
-        shift = work.tile([N, 1], FP32, name="shift")
-        nc.scalar.mul(shift[:], smallest[:], INV_SQRT_C)
 
-        expo = work.tile([N, R], BF16, name="expo")
-        block_totals = work.tile([N, R_BLOCKS], FP32, name="block_totals")
+        shifted = [banks.tile([P, N], FP32, name="shifted%d" % b, tag="bank") for b in range(R_BLOCKS)]
         for b in range(R_BLOCKS):
-            nc.scalar.activation(
-                expo[:, b * P : (b + 1) * P],
-                dist[:, b * P : (b + 1) * P],
-                FUNC.Exp,
-                bias=shift[:],
-                scale=-INV_SQRT_C,
-                accum_out=block_totals[:, b : b + 1],
+            nc.tensor.matmul(
+                shifted[b][:], dist[:, b * P : (b + 1) * P], identity_f32[:], is_transpose=True, start=True, stop=False
             )
 
-        expo_t = work.tile([P, R_BLOCKS, N], BF16, name="expo_t")
+        smallest = work.tile([N, 1], BF16, name="smallest")
+        with nc.allow_low_precision(reason="the shift of a softmax need not be the exact minimum"):
+            nc.vector.tensor_reduce(smallest[:], dist[:], AXIS.X, ALU.min)
+        smallest_diag = work.tile([N, N], BF16, name="smallest_diag")
+        nc.vector.tensor_scalar_mul(smallest_diag[:], identity[:], smallest[:])
         for b in range(R_BLOCKS):
-            expo_t_ps = banks.tile([P, N], BF16, name="expo_t_ps", tag="bank")
-            nc.tensor.transpose(expo_t_ps[:], expo[:, b * P : (b + 1) * P], identity[:])
-            nc.vector.tensor_copy(expo_t[:, b, :], expo_t_ps[:])
+            nc.tensor.matmul(shifted[b][:], minus_ones[:], smallest_diag[:], start=False, stop=True)
 
-        acc = [banks.tile([P, N], FP32, name="acc%d" % e, tag="bank") for e in range(E_BLOCKS)]
-        for b in range(HALF_BLOCKS):
-            for e in range(E_BLOCKS):
-                nc.tensor.matmul(acc[e][:], mv_sb[:, b, e * P : (e + 1) * P], expo_t[:, b, :], start=(b == 0), stop=False)
-
+        shift = work.tile([N, 1], FP32, name="shift")
+        nc.scalar.mul(shift[:], smallest[:], INV_SQRT_C)
+        expo = work.tile([N, R], BF16, name="expo")
         total = work.tile([N, 1], FP32, name="total")
-        nc.vector.tensor_reduce(total[:], block_totals[:], AXIS.X, ALU.add)
+        nc.scalar.activation(expo[:], dist[:], FUNC.Exp, bias=shift[:], scale=-INV_SQRT_C, accum_out=total[:])
+
         inv_total = work.tile([N, 1], FP32, name="inv_total")
         nc.vector.reciprocal(inv_total[:], total[:])
         inv_cols = work.tile([N, P], FP32, name="inv_cols")
         nc.vector.tensor_copy(inv_cols[:], inv_total[:].to_broadcast([N, P]))
+
+        expo_t = work.tile([P, R_BLOCKS, N], BF16, name="expo_t")
+        acc = [banks.tile([P, N], FP32, name="acc%d" % e, tag="bank") for e in range(E_BLOCKS)]
         inv_rows_ps = banks.tile([P, N], FP32, name="inv_rows_ps", tag="bank")
-        nc.tensor.transpose(inv_rows_ps[:], inv_cols[:], identity_f32[:])
+        for b in range(R_BLOCKS):
+            nc.scalar.activation(expo_t[:, b, :], shifted[b][:], FUNC.Exp, scale=-INV_SQRT_C)
+            for e in range(E_BLOCKS):
+                nc.tensor.matmul(
+                    acc[e][:], mv_sb[:, b, e * P : (e + 1) * P], expo_t[:, b, :], start=(b == 0), stop=(b == R_BLOCKS - 1)
+                )
+            if b == 0:
+                nc.tensor.transpose(inv_rows_ps[:], inv_cols[:], identity_f32[:])
         inv_rows = work.tile([P, N], FP32, name="inv_rows")
-        nc.scalar.copy(inv_rows[:], inv_rows_ps[:])
+        nc.vector.tensor_copy(inv_rows[:], inv_rows_ps[:])
 
         for e in range(E_BLOCKS):
-            for b in range(HALF_BLOCKS, R_BLOCKS):
-                nc.tensor.matmul(
-                    acc[e][:], mv_sb[:, b, e * P : (e + 1) * P], expo_t[:, b, :], start=False, stop=(b == R_BLOCKS - 1)
-                )
             block = staged.tile([P, N], FP32, name="block")
             nc.vector.tensor_tensor(block[:], acc[e][:], inv_rows[:], ALU.mult)
             queue = nc.sync if e % 2 == 0 else nc.scalar

@@ -14,6 +14,7 @@ P = 128
 C, S, N, R, E = 128, 512, 128, 512, 512
 R_BLOCKS = R // P
 E_BLOCKS = E // P
+HALF_BLOCKS = R_BLOCKS // 2
 PSUM_BANKS = 8
 INV_SQRT_C = 1.0 / math.sqrt(C)
 
@@ -102,20 +103,24 @@ def tile_vidsam_kernel(tc, x, sel, mk, shrink, mv, offs, out):
         nc.vector.tensor_copy(inv_cols[:], inv_total[:].to_broadcast([N, P]))
 
         expo_t = work.tile([P, R_BLOCKS, N], BF16, name="expo_t")
-        acc = [banks.tile([P, N], FP32, name="acc%d" % e, tag="bank") for e in range(E_BLOCKS)]
-        inv_rows_ps = banks.tile([P, N], FP32, name="inv_rows_ps", tag="bank")
         for b in range(R_BLOCKS):
             nc.scalar.activation(expo_t[:, b, :], shifted[b][:], FUNC.Exp, scale=-INV_SQRT_C)
+
+        acc = [banks.tile([P, N], FP32, name="acc%d" % e, tag="bank") for e in range(E_BLOCKS)]
+        inv_rows_ps = banks.tile([P, N], FP32, name="inv_rows_ps", tag="bank")
+        for b in range(HALF_BLOCKS):
             for e in range(E_BLOCKS):
-                nc.tensor.matmul(
-                    acc[e][:], mv_sb[:, b, e * P : (e + 1) * P], expo_t[:, b, :], start=(b == 0), stop=(b == R_BLOCKS - 1)
-                )
+                nc.tensor.matmul(acc[e][:], mv_sb[:, b, e * P : (e + 1) * P], expo_t[:, b, :], start=(b == 0), stop=False)
             if b == 0:
                 nc.tensor.transpose(inv_rows_ps[:], inv_cols[:], identity_f32[:])
         inv_rows = work.tile([P, N], FP32, name="inv_rows")
         nc.vector.tensor_copy(inv_rows[:], inv_rows_ps[:])
 
         for e in range(E_BLOCKS):
+            for b in range(HALF_BLOCKS, R_BLOCKS):
+                nc.tensor.matmul(
+                    acc[e][:], mv_sb[:, b, e * P : (e + 1) * P], expo_t[:, b, :], start=False, stop=(b == R_BLOCKS - 1)
+                )
             block = staged.tile([P, N], FP32, name="block")
             nc.vector.tensor_tensor(block[:], acc[e][:], inv_rows[:], ALU.mult)
             queue = nc.sync if e % 2 == 0 else nc.scalar

@@ -48,8 +48,6 @@ def tile_vidsam_kernel(tc, x, sel, mk, shrink, mv, offs, out):
         make_identity(nc, identity_f32[:])
         ones = held.tile([C, 1], BF16, name="ones")
         nc.gpsimd.memset(ones[:], 1.0)
-        minus_ones = held.tile([N, P], BF16, name="minus_ones")
-        nc.gpsimd.memset(minus_ones[:], -1.0)
         warm = held.tile([P, 1], FP32, name="warm")
         nc.vector.memset(warm[:], 0.0)
         nc.scalar.activation(warm[:], warm[:], FUNC.Exp)
@@ -83,16 +81,14 @@ def tile_vidsam_kernel(tc, x, sel, mk, shrink, mv, offs, out):
                 shifted[b][:], dist[:, b * P : (b + 1) * P], identity_f32[:], is_transpose=True, start=True, stop=False
             )
 
-        smallest = work.tile([N, 1], BF16, name="smallest")
+        minus_smallest = work.tile([N, 1], BF16, name="minus_smallest")
         with nc.allow_low_precision(reason="the shift of a softmax need not be the exact minimum"):
-            nc.vector.tensor_reduce(smallest[:], dist[:], AXIS.X, ALU.min)
-        smallest_diag = work.tile([N, N], BF16, name="smallest_diag")
-        nc.vector.tensor_scalar_mul(smallest_diag[:], identity[:], smallest[:])
+            nc.vector.tensor_reduce(minus_smallest[:], dist[:], AXIS.X, ALU.min, negate=True)
         for b in range(R_BLOCKS):
-            nc.tensor.matmul(shifted[b][:], minus_ones[:], smallest_diag[:], start=False, stop=True)
+            nc.tensor.matmul(shifted[b][:], minus_smallest[:].to_broadcast([N, P]), identity[:], start=False, stop=True)
 
         shift = work.tile([N, 1], FP32, name="shift")
-        nc.scalar.mul(shift[:], smallest[:], INV_SQRT_C)
+        nc.scalar.mul(shift[:], minus_smallest[:], -INV_SQRT_C)
         expo = work.tile([N, R], BF16, name="expo")
         total = work.tile([N, 1], FP32, name="total")
         nc.scalar.activation(expo[:], dist[:], FUNC.Exp, bias=shift[:], scale=-INV_SQRT_C, accum_out=total[:])

import math

import concourse.mybir as mybir
from concourse.masks import make_identity

FP32 = mybir.dt.float32
BF16 = mybir.dt.bfloat16
U16 = mybir.dt.uint16
ALU = mybir.AluOpType
FUNC = mybir.ActivationFunctionType
AXIS = mybir.AxisListType

P = 128
C, S, N, R, E = 128, 512, 128, 512, 512
R_BLOCKS = R // P
E_BLOCKS = E // P
HALF_BLOCKS = R_BLOCKS // 2
PSUM_BANKS = 8
INV_SQRT_C = 1.0 / math.sqrt(C)

FLOPS = 2 * (2 * C) * R * N + 2 * C * N + 2 * R * E * N


def tile_vidsam_kernel(tc, x, sel, mk, shrink, mv, offs, out):
    nc = tc.nc
    with (
        tc.tile_pool(name="held", bufs=1) as held,
        tc.tile_pool(name="work", bufs=1) as work,
        tc.tile_pool(name="staged", bufs=E_BLOCKS) as staged,
        tc.psum_pool(name="banks", bufs=PSUM_BANKS) as banks,
    ):
        offsets = held.tile([P, N // 16], U16, name="offsets")
        nc.sync.dma_start(offsets[:], offs)
        x_sb = held.tile([C, S], FP32, name="x_sb")
        nc.sync.dma_start(x_sb[:], x)
        mk_sb = held.tile([C, R], BF16, name="mk_sb")
        nc.scalar.dma_start(mk_sb[:], mk)
        sel_sb = held.tile([C, N], FP32, name="sel_sb")
        nc.scalar.dma_start(sel_sb[:], sel)
        shrink_rows = held.tile([P, R], FP32, name="shrink_rows")
        nc.sync.dma_start(shrink_rows[:], shrink.rearrange("r one -> (r one)").partition_broadcast(P))
        mv_sb = held.tile([P, R_BLOCKS, E], BF16, name="mv_sb")
        nc.sync.dma_start(mv_sb[:], mv.rearrange("(b p) e -> p b e", p=P))

        identity = held.tile([P, P], BF16, name="identity")
        make_identity(nc, identity[:])
        identity_f32 = held.tile([P, P], FP32, name="identity_f32")
        make_identity(nc, identity_f32[:])
        ones = held.tile([C, 1], BF16, name="ones")
        nc.gpsimd.memset(ones[:], 1.0)
        warm = held.tile([P, 1], FP32, name="warm")
        nc.vector.memset(warm[:], 0.0)
        nc.scalar.activation(warm[:], warm[:], FUNC.Exp)

        mk_sq = work.tile([C, R], BF16, name="mk_sq")
        nc.vector.tensor_tensor(mk_sq[:], mk_sb[:], mk_sb[:], ALU.mult)
        sel_bf = work.tile([C, N], BF16, name="sel_bf")
        nc.vector.tensor_copy(sel_bf[:], sel_sb[:])

        u = work.tile([C, N], FP32, name="u")
        nc.vector.tensor_tensor(u[:], x_sb[:].indirect(offsets[:]), sel_sb[:], ALU.mult)
        u_minus2 = work.tile([C, N], BF16, name="u_minus2")
        nc.vector.tensor_scalar_mul(u_minus2[:], u[:], -2.0)
        xu = work.tile([C, N], FP32, name="xu")
        nc.vector.tensor_tensor(xu[:], x_sb[:].indirect(offsets[:]), u[:], ALU.mult)
        xu_bf = work.tile([C, N], BF16, name="xu_bf")
        nc.vector.tensor_copy(xu_bf[:], xu[:])

        cross = banks.tile([N, R], FP32, name="cross", tag="bank")
        nc.tensor.matmul(cross[:], sel_bf[:], mk_sq[:], start=True, stop=False)
        nc.tensor.matmul(cross[:], u_minus2[:], mk_sb[:], start=False, stop=True)
        bsq = banks.tile([N, 1], FP32, name="bsq", tag="bank")
        nc.tensor.matmul(bsq[:], xu_bf[:], ones[:], start=True, stop=True)

        dist = work.tile([N, R], FP32, name="dist")
        nc.vector.scalar_tensor_tensor(dist[:], cross[:], bsq[:], shrink_rows[:], ALU.add, ALU.mult)

        shifted = [banks.tile([P, N], FP32, name="shifted%d" % b, tag="bank") for b in range(R_BLOCKS)]
        for b in range(R_BLOCKS):
            nc.tensor.matmul(
                shifted[b][:], dist[:, b * P : (b + 1) * P], identity_f32[:], is_transpose=True, start=True, stop=False
            )

        minus_smallest = work.tile([N, 1], BF16, name="minus_smallest")
        with nc.allow_low_precision(reason="the shift of a softmax need not be the exact minimum"):
            nc.vector.tensor_reduce(minus_smallest[:], dist[:], AXIS.X, ALU.min, negate=True)
        for b in range(R_BLOCKS):
            nc.tensor.matmul(shifted[b][:], minus_smallest[:].to_broadcast([N, P]), identity[:], start=False, stop=True)

        shift = work.tile([N, 1], FP32, name="shift")
        nc.scalar.mul(shift[:], minus_smallest[:], -INV_SQRT_C)
        expo = work.tile([N, R], BF16, name="expo")
        total = work.tile([N, 1], FP32, name="total")
        nc.scalar.activation(expo[:], dist[:], FUNC.Exp, bias=shift[:], scale=-INV_SQRT_C, accum_out=total[:])

        inv_total = work.tile([N, 1], FP32, name="inv_total")
        nc.vector.reciprocal(inv_total[:], total[:])
        inv_cols = work.tile([N, P], FP32, name="inv_cols")
        nc.vector.tensor_copy(inv_cols[:], inv_total[:].to_broadcast([N, P]))

        expo_t = work.tile([P, R_BLOCKS, N], BF16, name="expo_t")
        for b in range(R_BLOCKS):
            nc.scalar.activation(expo_t[:, b, :], shifted[b][:], FUNC.Exp, scale=-INV_SQRT_C)

        acc = [banks.tile([P, N], FP32, name="acc%d" % e, tag="bank") for e in range(E_BLOCKS)]
        inv_rows_ps = banks.tile([P, N], FP32, name="inv_rows_ps", tag="bank")
        for b in range(HALF_BLOCKS):
            for e in range(E_BLOCKS):
                nc.tensor.matmul(acc[e][:], mv_sb[:, b, e * P : (e + 1) * P], expo_t[:, b, :], start=(b == 0), stop=False)
            if b == 0:
                nc.tensor.transpose(inv_rows_ps[:], inv_cols[:], identity_f32[:])
        inv_rows = work.tile([P, N], FP32, name="inv_rows")
        nc.vector.tensor_copy(inv_rows[:], inv_rows_ps[:])

        for e in range(E_BLOCKS):
            for b in range(HALF_BLOCKS, R_BLOCKS):
                nc.tensor.matmul(
                    acc[e][:], mv_sb[:, b, e * P : (e + 1) * P], expo_t[:, b, :], start=False, stop=(b == R_BLOCKS - 1)
                )
            block = staged.tile([P, N], FP32, name="block")
            nc.vector.tensor_tensor(block[:], acc[e][:], inv_rows[:], ALU.mult)
            queue = nc.sync if e % 2 == 0 else nc.scalar
            queue.dma_start(out[e * P : (e + 1) * P, :], block[:])
